import numpy as np
import ml_dtypes

BF16 = ml_dtypes.bfloat16


def bf(x):
    return np.asarray(x, np.float32).astype(BF16)


def f32(x):
    return np.asarray(x, np.float32)


def f64(x):
    return np.asarray(x).astype(np.float64)


def striped(idx):
    return np.tile(idx.reshape(-1, 16).T, (8, 1))


C, I, S, N, GRID_SIZE, SPLINE_ORDER = 128, 128, 512, 128, 5, 3
K = GRID_SIZE + SPLINE_ORDER
GRID_LO, GRID_HI = -1.0, 1.0
CENTERS = np.linspace(GRID_LO, GRID_HI, GRID_SIZE + 2 * SPLINE_ORDER + 1)[SPLINE_ORDER:SPLINE_ORDER + K]
SPACING = (GRID_HI - GRID_LO) / GRID_SIZE + 1e-06


def setup_inputs():
    return {"base": f32(np.random.standard_normal((C, S))), "x": f32(np.random.standard_normal((I, N))), "coeff": f32(0.5 * np.random.standard_normal((K, I, C))), "ew": f32(0.1 * np.random.standard_normal((I, C))), "bw": f32(1.0 + 0.1 * np.random.standard_normal((I, C))), "bb": f32(0.1 * np.random.standard_normal((I, C))), "offs": striped(np.random.permutation(S)[:N])}


def reference(base, x, coeff, ew, bw, bb, offs):
    idx = offs[:16].T.reshape(-1)
    x, ew = f64(x), f64(ew)
    silu = x / (1.0 + np.exp(-x))
    a = (ew * f64(bw)).T @ silu + np.sum(ew * f64(bb), axis=0)[:, None]
    z = (x[None, :, :] - CENTERS[:, None, None]) / SPACING
    basis = np.exp(-0.5 * z * z)
    wk = ew[None, :, :] * f64(coeff)
    b = wk.reshape(K * I, C).T @ basis.reshape(K * I, N)
    out = f64(base).copy()
    out[:, idx] = a + b
    return out

@@ -1,0 +1,84 @@
+import concourse.mybir as mybir
+
+F32, BF16, U16 = mybir.dt.float32, mybir.dt.bfloat16, mybir.dt.uint16
+ALU = mybir.AluOpType
+ACT = mybir.ActivationFunctionType
+
+C, I, S, N, K = 128, 128, 512, 128, 8
+SPACING = 0.400001
+CENTERS = [(2 * k - 5) / 11 for k in range(K)]
+HALF_INV_VAR = 0.5 / (SPACING * SPACING)
+
+FLOPS = 2 * C * N * I * (K + 1)
+
+
+def tile_kanlayer_kernel(tc, base, x, coeff, ew, bw, bb, offs, out):
+    nc = tc.nc
+    with (
+        tc.tile_pool(name="held", bufs=1) as held,
+        tc.psum_pool(name="psum", bufs=1) as psum,
+    ):
+        offsets = held.tile([128, N // 16], U16, name="offsets")
+        nc.sync.dma_start(offsets[:], offs)
+        x_sb = held.tile([I, N], F32, name="x_sb")
+        nc.sync.dma_start(x_sb[:], x)
+        ew_sb = held.tile([I, C], F32, name="ew_sb")
+        nc.scalar.dma_start(ew_sb[:], ew)
+        coeff_sb = held.tile([I, K, C], F32, name="coeff_sb")
+        coeff_ikc = coeff.rearrange("k i c -> i k c")
+        nc.sync.dma_start(coeff_sb[:, 0 : K // 2, :], coeff_ikc[:, 0 : K // 2, :])
+        nc.scalar.dma_start(coeff_sb[:, K // 2 : K, :], coeff_ikc[:, K // 2 : K, :])
+        bw_sb = held.tile([I, C], F32, name="bw_sb")
+        nc.sync.dma_start(bw_sb[:], bw)
+        bb_sb = held.tile([I, C], F32, name="bb_sb")
+        nc.scalar.dma_start(bb_sb[:], bb)
+        window = held.tile([C, S], F32, name="window")
+        nc.gpsimd.dma_start(window[:], base)
+
+        ones = held.tile([I, N], BF16, name="ones")
+        nc.gpsimd.memset(ones[:], 1.0)
+
+        tanh_half = held.tile([I, N], F32, name="tanh_half")
+        nc.scalar.activation(tanh_half[:], x_sb[:], ACT.Tanh, scale=0.5)
+        sigmoid = held.tile([I, N], F32, name="sigmoid")
+        nc.vector.tensor_scalar(sigmoid[:], tanh_half[:], 0.5, 0.5, ALU.mult, ALU.add)
+        silu = held.tile([I, N], BF16, name="silu")
+        nc.vector.tensor_tensor(silu[:], x_sb[:], sigmoid[:], ALU.mult)
+
+        bumps = held.tile([I, K, N], BF16, name="bumps")
+        for k in range(K):
+            center = CENTERS[k]
+            cross = held.tile([I, N], F32, name=f"cross{k}")
+            nc.vector.scalar_tensor_tensor(
+                cross[:], x_sb[:], 2.0 * center, x_sb[:], ALU.subtract, ALU.mult
+            )
+            nc.scalar.activation(
+                bumps[:, k, :], cross[:], ACT.Exp,
+                bias=-HALF_INV_VAR * center * center, scale=-HALF_INV_VAR,
+            )
+
+        ew_bw = held.tile([I, C], BF16, name="ew_bw")
+        nc.vector.tensor_tensor(ew_bw[:], ew_sb[:], bw_sb[:], ALU.mult)
+        ew_bb = held.tile([I, C], BF16, name="ew_bb")
+        nc.vector.tensor_tensor(ew_bb[:], ew_sb[:], bb_sb[:], ALU.mult)
+        ew_coeff = held.tile([I, K, C], BF16, name="ew_coeff")
+        for k in range(K):
+            nc.vector.tensor_tensor(ew_coeff[:, k, :], coeff_sb[:, k, :], ew_sb[:], ALU.mult)
+
+        a_ps = psum.tile([C, N], F32, name="a_ps")
+        nc.tensor.matmul(a_ps[:], ew_bw[:], silu[:], start=True, stop=False)
+        nc.tensor.matmul(a_ps[:], ew_bb[:], ones[:], start=False, stop=True)
+        a_sb = held.tile([C, N], F32, name="a_sb")
+        nc.scalar.copy(a_sb[:], a_ps[:])
+
+        b_ps = psum.tile([C, N], F32, name="b_ps")
+        for k in range(K):
+            nc.tensor.matmul(
+                b_ps[:], ew_coeff[:, k, :], bumps[:, k, :], start=(k == 0), stop=(k == K - 1)
+            )
+
+        b_sb = held.tile([C, N], F32, name="b_sb")
+        nc.vector.tensor_copy(b_sb[:], b_ps[:])
+
+        nc.vector.tensor_tensor(window[:].indirect(offsets[:]), a_sb[:], b_sb[:], ALU.add)
+        nc.sync.dma_start(out, window[:])

@@ -1,3 +1,5 @@
+import math
+
 import concourse.mybir as mybir
 
 F32, BF16, U16 = mybir.dt.float32, mybir.dt.bfloat16, mybir.dt.uint16
@@ -7,7 +9,8 @@ ACT = mybir.ActivationFunctionType
 C, I, S, N, K = 128, 128, 512, 128, 8
 SPACING = 0.400001
 CENTERS = [(2 * k - 5) / 11 for k in range(K)]
-HALF_INV_VAR = 0.5 / (SPACING * SPACING)
+Z_SCALE = 1.0 / (SPACING * math.sqrt(2.0))
+K_PIECE = 2
 
 FLOPS = 2 * C * N * I * (K + 1)
 
@@ -18,22 +21,24 @@ def tile_kanlayer_kernel(tc, base, x, coeff, ew, bw, bb, offs, out):
         tc.tile_pool(name="held", bufs=1) as held,
         tc.psum_pool(name="psum", bufs=1) as psum,
     ):
-        offsets = held.tile([128, N // 16], U16, name="offsets")
-        nc.sync.dma_start(offsets[:], offs)
         x_sb = held.tile([I, N], F32, name="x_sb")
-        nc.sync.dma_start(x_sb[:], x)
+        nc.scalar.dma_start(x_sb[:], x)
         ew_sb = held.tile([I, C], F32, name="ew_sb")
-        nc.scalar.dma_start(ew_sb[:], ew)
-        coeff_sb = held.tile([I, K, C], F32, name="coeff_sb")
-        coeff_ikc = coeff.rearrange("k i c -> i k c")
-        nc.sync.dma_start(coeff_sb[:, 0 : K // 2, :], coeff_ikc[:, 0 : K // 2, :])
-        nc.scalar.dma_start(coeff_sb[:, K // 2 : K, :], coeff_ikc[:, K // 2 : K, :])
+        nc.sync.dma_start(ew_sb[:], ew)
         bw_sb = held.tile([I, C], F32, name="bw_sb")
         nc.sync.dma_start(bw_sb[:], bw)
         bb_sb = held.tile([I, C], F32, name="bb_sb")
-        nc.scalar.dma_start(bb_sb[:], bb)
+        nc.sync.dma_start(bb_sb[:], bb)
+        coeff_ikc = coeff.rearrange("k i c -> i k c")
+        coeff_sb = []
+        for k0 in range(0, K, K_PIECE):
+            piece = held.tile([I, K_PIECE, C], F32, name=f"coeff_sb{k0}")
+            nc.sync.dma_start(piece[:], coeff_ikc[:, k0 : k0 + K_PIECE, :])
+            coeff_sb.append(piece)
+        offsets = held.tile([128, N // 16], U16, name="offsets")
+        nc.sync.dma_start(offsets[:], offs)
         window = held.tile([C, S], F32, name="window")
-        nc.gpsimd.dma_start(window[:], base)
+        nc.sync.dma_start(window[:], base)
 
         ones = held.tile([I, N], BF16, name="ones")
         nc.gpsimd.memset(ones[:], 1.0)
@@ -45,38 +50,29 @@ def tile_kanlayer_kernel(tc, base, x, coeff, ew, bw, bb, offs, out):
         silu = held.tile([I, N], BF16, name="silu")
         nc.vector.tensor_tensor(silu[:], x_sb[:], sigmoid[:], ALU.mult)
 
-        bumps = held.tile([I, K, N], BF16, name="bumps")
-        for k in range(K):
-            center = CENTERS[k]
-            cross = held.tile([I, N], F32, name=f"cross{k}")
-            nc.vector.scalar_tensor_tensor(
-                cross[:], x_sb[:], 2.0 * center, x_sb[:], ALU.subtract, ALU.mult
-            )
-            nc.scalar.activation(
-                bumps[:, k, :], cross[:], ACT.Exp,
-                bias=-HALF_INV_VAR * center * center, scale=-HALF_INV_VAR,
-            )
-
         ew_bw = held.tile([I, C], BF16, name="ew_bw")
         nc.vector.tensor_tensor(ew_bw[:], ew_sb[:], bw_sb[:], ALU.mult)
         ew_bb = held.tile([I, C], BF16, name="ew_bb")
         nc.vector.tensor_tensor(ew_bb[:], ew_sb[:], bb_sb[:], ALU.mult)
-        ew_coeff = held.tile([I, K, C], BF16, name="ew_coeff")
-        for k in range(K):
-            nc.vector.tensor_tensor(ew_coeff[:, k, :], coeff_sb[:, k, :], ew_sb[:], ALU.mult)
-
         a_ps = psum.tile([C, N], F32, name="a_ps")
         nc.tensor.matmul(a_ps[:], ew_bw[:], silu[:], start=True, stop=False)
         nc.tensor.matmul(a_ps[:], ew_bb[:], ones[:], start=False, stop=True)
         a_sb = held.tile([C, N], F32, name="a_sb")
-        nc.scalar.copy(a_sb[:], a_ps[:])
+        nc.vector.tensor_copy(a_sb[:], a_ps[:])
 
         b_ps = psum.tile([C, N], F32, name="b_ps")
         for k in range(K):
-            nc.tensor.matmul(
-                b_ps[:], ew_coeff[:, k, :], bumps[:, k, :], start=(k == 0), stop=(k == K - 1)
+            z_squared = held.tile([I, N], F32, name=f"z_squared{k}")
+            nc.scalar.activation(
+                z_squared[:], x_sb[:], ACT.Square, bias=-Z_SCALE * CENTERS[k], scale=Z_SCALE
             )
-
+            bump = held.tile([I, N], BF16, name=f"bump{k}")
+            nc.scalar.activation(bump[:], z_squared[:], ACT.Exp, scale=-1.0)
+            ew_coeff = held.tile([I, C], BF16, name=f"ew_coeff{k}")
+            nc.vector.tensor_tensor(
+                ew_coeff[:], coeff_sb[k // K_PIECE][:, k % K_PIECE, :], ew_sb[:], ALU.mult
+            )
+            nc.tensor.matmul(b_ps[:], ew_coeff[:], bump[:], start=(k == 0), stop=(k == K - 1))
         b_sb = held.tile([C, N], F32, name="b_sb")
         nc.vector.tensor_copy(b_sb[:], b_ps[:])
 

@@ -11,6 +11,7 @@ SPACING = 0.400001
 CENTERS = [(2 * k - 5) / 11 for k in range(K)]
 Z_SCALE = 1.0 / (SPACING * math.sqrt(2.0))
 K_PIECE = 2
+K_SCALAR_SQUARES = K - 2
 
 FLOPS = 2 * C * N * I * (K + 1)
 
@@ -50,6 +51,12 @@ def tile_kanlayer_kernel(tc, base, x, coeff, ew, bw, bb, offs, out):
         silu = held.tile([I, N], BF16, name="silu")
         nc.vector.tensor_tensor(silu[:], x_sb[:], sigmoid[:], ALU.mult)
 
+        z_squared = [held.tile([I, N], F32, name=f"z_squared{k}") for k in range(K)]
+        for k in range(K_SCALAR_SQUARES, K):
+            z = held.tile([I, N], F32, name=f"z{k}")
+            nc.vector.tensor_scalar(z[:], x_sb[:], CENTERS[k], Z_SCALE, ALU.subtract, ALU.mult)
+            nc.vector.tensor_tensor(z_squared[k][:], z[:], z[:], ALU.mult)
+
         ew_bw = held.tile([I, C], BF16, name="ew_bw")
         nc.vector.tensor_tensor(ew_bw[:], ew_sb[:], bw_sb[:], ALU.mult)
         ew_bb = held.tile([I, C], BF16, name="ew_bb")
@@ -62,12 +69,12 @@ def tile_kanlayer_kernel(tc, base, x, coeff, ew, bw, bb, offs, out):
 
         b_ps = psum.tile([C, N], F32, name="b_ps")
         for k in range(K):
-            z_squared = held.tile([I, N], F32, name=f"z_squared{k}")
-            nc.scalar.activation(
-                z_squared[:], x_sb[:], ACT.Square, bias=-Z_SCALE * CENTERS[k], scale=Z_SCALE
-            )
+            if k < K_SCALAR_SQUARES:
+                nc.scalar.activation(
+                    z_squared[k][:], x_sb[:], ACT.Square, bias=-Z_SCALE * CENTERS[k], scale=Z_SCALE
+                )
             bump = held.tile([I, N], BF16, name=f"bump{k}")
-            nc.scalar.activation(bump[:], z_squared[:], ACT.Exp, scale=-1.0)
+            nc.scalar.activation(bump[:], z_squared[k][:], ACT.Exp, scale=-1.0)
             ew_coeff = held.tile([I, C], BF16, name=f"ew_coeff{k}")
             nc.vector.tensor_tensor(
                 ew_coeff[:], coeff_sb[k // K_PIECE][:, k % K_PIECE, :], ew_sb[:], ALU.mult

@@ -11,7 +11,7 @@ SPACING = 0.400001
 CENTERS = [(2 * k - 5) / 11 for k in range(K)]
 Z_SCALE = 1.0 / (SPACING * math.sqrt(2.0))
 K_PIECE = 2
-K_SCALAR_SQUARES = K - 2
+K_VECTOR_SQUARES = 2
 
 FLOPS = 2 * C * N * I * (K + 1)
 
@@ -23,13 +23,13 @@ def tile_kanlayer_kernel(tc, base, x, coeff, ew, bw, bb, offs, out):
         tc.psum_pool(name="psum", bufs=1) as psum,
     ):
         x_sb = held.tile([I, N], F32, name="x_sb")
-        nc.scalar.dma_start(x_sb[:], x)
+        nc.sync.dma_start(x_sb[:], x)
+        bw_sb = held.tile([I, C], F32, name="bw_sb")
+        nc.scalar.dma_start(bw_sb[:], bw)
         ew_sb = held.tile([I, C], F32, name="ew_sb")
         nc.sync.dma_start(ew_sb[:], ew)
-        bw_sb = held.tile([I, C], F32, name="bw_sb")
-        nc.sync.dma_start(bw_sb[:], bw)
         bb_sb = held.tile([I, C], F32, name="bb_sb")
-        nc.sync.dma_start(bb_sb[:], bb)
+        nc.scalar.dma_start(bb_sb[:], bb)
         coeff_ikc = coeff.rearrange("k i c -> i k c")
         coeff_sb = []
         for k0 in range(0, K, K_PIECE):
@@ -44,32 +44,31 @@ def tile_kanlayer_kernel(tc, base, x, coeff, ew, bw, bb, offs, out):
         ones = held.tile([I, N], BF16, name="ones")
         nc.gpsimd.memset(ones[:], 1.0)
 
+        z_squared = [held.tile([I, N], F32, name=f"z_squared{k}") for k in range(K)]
+        vector_squares = range(K - K_VECTOR_SQUARES, K)
+        z = {k: held.tile([I, N], F32, name=f"z{k}") for k in vector_squares}
+        for k in vector_squares:
+            nc.vector.tensor_scalar(z[k][:], x_sb[:], CENTERS[k], Z_SCALE, ALU.subtract, ALU.mult)
+        for k in vector_squares:
+            nc.vector.tensor_tensor(z_squared[k][:], z[k][:], z[k][:], ALU.mult)
+
         tanh_half = held.tile([I, N], F32, name="tanh_half")
         nc.scalar.activation(tanh_half[:], x_sb[:], ACT.Tanh, scale=0.5)
-        sigmoid = held.tile([I, N], F32, name="sigmoid")
-        nc.vector.tensor_scalar(sigmoid[:], tanh_half[:], 0.5, 0.5, ALU.mult, ALU.add)
-        silu = held.tile([I, N], BF16, name="silu")
-        nc.vector.tensor_tensor(silu[:], x_sb[:], sigmoid[:], ALU.mult)
-
-        z_squared = [held.tile([I, N], F32, name=f"z_squared{k}") for k in range(K)]
-        for k in range(K_SCALAR_SQUARES, K):
-            z = held.tile([I, N], F32, name=f"z{k}")
-            nc.vector.tensor_scalar(z[:], x_sb[:], CENTERS[k], Z_SCALE, ALU.subtract, ALU.mult)
-            nc.vector.tensor_tensor(z_squared[k][:], z[:], z[:], ALU.mult)
-
         ew_bw = held.tile([I, C], BF16, name="ew_bw")
         nc.vector.tensor_tensor(ew_bw[:], ew_sb[:], bw_sb[:], ALU.mult)
         ew_bb = held.tile([I, C], BF16, name="ew_bb")
         nc.vector.tensor_tensor(ew_bb[:], ew_sb[:], bb_sb[:], ALU.mult)
+        sigmoid = held.tile([I, N], F32, name="sigmoid")
+        nc.vector.tensor_scalar(sigmoid[:], tanh_half[:], 0.5, 0.5, ALU.mult, ALU.add)
+        silu = held.tile([I, N], BF16, name="silu")
+        nc.vector.tensor_tensor(silu[:], x_sb[:], sigmoid[:], ALU.mult)
         a_ps = psum.tile([C, N], F32, name="a_ps")
-        nc.tensor.matmul(a_ps[:], ew_bw[:], silu[:], start=True, stop=False)
-        nc.tensor.matmul(a_ps[:], ew_bb[:], ones[:], start=False, stop=True)
-        a_sb = held.tile([C, N], F32, name="a_sb")
-        nc.vector.tensor_copy(a_sb[:], a_ps[:])
+        nc.tensor.matmul(a_ps[:], ew_bb[:], ones[:], start=True, stop=False)
+        nc.tensor.matmul(a_ps[:], ew_bw[:], silu[:], start=False, stop=True)
 
         b_ps = psum.tile([C, N], F32, name="b_ps")
         for k in range(K):
-            if k < K_SCALAR_SQUARES:
+            if k not in vector_squares:
                 nc.scalar.activation(
                     z_squared[k][:], x_sb[:], ACT.Square, bias=-Z_SCALE * CENTERS[k], scale=Z_SCALE
                 )
@@ -80,6 +79,9 @@ def tile_kanlayer_kernel(tc, base, x, coeff, ew, bw, bb, offs, out):
                 ew_coeff[:], coeff_sb[k // K_PIECE][:, k % K_PIECE, :], ew_sb[:], ALU.mult
             )
             nc.tensor.matmul(b_ps[:], ew_coeff[:], bump[:], start=(k == 0), stop=(k == K - 1))
+
+        a_sb = held.tile([C, N], F32, name="a_sb")
+        nc.vector.tensor_copy(a_sb[:], a_ps[:])
         b_sb = held.tile([C, N], F32, name="b_sb")
         nc.vector.tensor_copy(b_sb[:], b_ps[:])
 

@@ -10,7 +10,7 @@ C, I, S, N, K = 128, 128, 512, 128, 8
 SPACING = 0.400001
 CENTERS = [(2 * k - 5) / 11 for k in range(K)]
 Z_SCALE = 1.0 / (SPACING * math.sqrt(2.0))
-K_PIECE = 2
+COEFF_PIECES = (3, 2, 2, 1)
 K_VECTOR_SQUARES = 2
 
 FLOPS = 2 * C * N * I * (K + 1)
@@ -32,10 +32,11 @@ def tile_kanlayer_kernel(tc, base, x, coeff, ew, bw, bb, offs, out):
         nc.scalar.dma_start(bb_sb[:], bb)
         coeff_ikc = coeff.rearrange("k i c -> i k c")
         coeff_sb = []
-        for k0 in range(0, K, K_PIECE):
-            piece = held.tile([I, K_PIECE, C], F32, name=f"coeff_sb{k0}")
-            nc.sync.dma_start(piece[:], coeff_ikc[:, k0 : k0 + K_PIECE, :])
-            coeff_sb.append(piece)
+        for bumps in COEFF_PIECES:
+            k0 = len(coeff_sb)
+            piece = held.tile([I, bumps, C], F32, name=f"coeff_piece{k0}")
+            nc.sync.dma_start(piece[:], coeff_ikc[:, k0 : k0 + bumps, :])
+            coeff_sb.extend(piece[:, m, :] for m in range(bumps))
         offsets = held.tile([128, N // 16], U16, name="offsets")
         nc.sync.dma_start(offsets[:], offs)
         window = held.tile([C, S], F32, name="window")
@@ -75,9 +76,7 @@ def tile_kanlayer_kernel(tc, base, x, coeff, ew, bw, bb, offs, out):
             bump = held.tile([I, N], BF16, name=f"bump{k}")
             nc.scalar.activation(bump[:], z_squared[k][:], ACT.Exp, scale=-1.0)
             ew_coeff = held.tile([I, C], BF16, name=f"ew_coeff{k}")
-            nc.vector.tensor_tensor(
-                ew_coeff[:], coeff_sb[k // K_PIECE][:, k % K_PIECE, :], ew_sb[:], ALU.mult
-            )
+            nc.vector.tensor_tensor(ew_coeff[:], coeff_sb[k], ew_sb[:], ALU.mult)
             nc.tensor.matmul(b_ps[:], ew_coeff[:], bump[:], start=(k == 0), stop=(k == K - 1))
 
         a_sb = held.tile([C, N], F32, name="a_sb")

@@ -10,7 +10,7 @@ C, I, S, N, K = 128, 128, 512, 128, 8
 SPACING = 0.400001
 CENTERS = [(2 * k - 5) / 11 for k in range(K)]
 Z_SCALE = 1.0 / (SPACING * math.sqrt(2.0))
-COEFF_PIECES = (3, 2, 2, 1)
+COEFF_PIECES = (1, 2, 2, 2, 1)
 K_VECTOR_SQUARES = 2
 
 FLOPS = 2 * C * N * I * (K + 1)

@@ -80,9 +80,9 @@ def tile_kanlayer_kernel(tc, base, x, coeff, ew, bw, bb, offs, out):
             nc.tensor.matmul(b_ps[:], ew_coeff[:], bump[:], start=(k == 0), stop=(k == K - 1))
 
         a_sb = held.tile([C, N], F32, name="a_sb")
-        nc.vector.tensor_copy(a_sb[:], a_ps[:])
+        nc.scalar.copy(a_sb[:], a_ps[:])
         b_sb = held.tile([C, N], F32, name="b_sb")
-        nc.vector.tensor_copy(b_sb[:], b_ps[:])
+        nc.scalar.copy(b_sb[:], b_ps[:])
 
         nc.vector.tensor_tensor(window[:].indirect(offsets[:]), a_sb[:], b_sb[:], ALU.add)
         nc.sync.dma_start(out, window[:])

@@ -24,12 +24,12 @@ def tile_kanlayer_kernel(tc, base, x, coeff, ew, bw, bb, offs, out):
     ):
         x_sb = held.tile([I, N], F32, name="x_sb")
         nc.sync.dma_start(x_sb[:], x)
-        bw_sb = held.tile([I, C], F32, name="bw_sb")
-        nc.scalar.dma_start(bw_sb[:], bw)
         ew_sb = held.tile([I, C], F32, name="ew_sb")
         nc.sync.dma_start(ew_sb[:], ew)
+        bw_sb = held.tile([I, C], F32, name="bw_sb")
+        nc.sync.dma_start(bw_sb[:], bw)
         bb_sb = held.tile([I, C], F32, name="bb_sb")
-        nc.scalar.dma_start(bb_sb[:], bb)
+        nc.sync.dma_start(bb_sb[:], bb)
         coeff_ikc = coeff.rearrange("k i c -> i k c")
         coeff_sb = []
         for bumps in COEFF_PIECES:
@@ -42,16 +42,15 @@ def tile_kanlayer_kernel(tc, base, x, coeff, ew, bw, bb, offs, out):
         window = held.tile([C, S], F32, name="window")
         nc.sync.dma_start(window[:], base)
 
-        ones = held.tile([I, N], BF16, name="ones")
-        nc.gpsimd.memset(ones[:], 1.0)
+        twos = held.tile([I, N], BF16, name="twos")
+        nc.gpsimd.memset(twos[:], 2.0)
 
-        z_squared = [held.tile([I, N], F32, name=f"z_squared{k}") for k in range(K)]
         vector_squares = range(K - K_VECTOR_SQUARES, K)
-        z = {k: held.tile([I, N], F32, name=f"z{k}") for k in vector_squares}
+        square_less_c2 = {k: held.tile([I, N], F32, name=f"square_less_c2_{k}") for k in vector_squares}
         for k in vector_squares:
-            nc.vector.tensor_scalar(z[k][:], x_sb[:], CENTERS[k], Z_SCALE, ALU.subtract, ALU.mult)
-        for k in vector_squares:
-            nc.vector.tensor_tensor(z_squared[k][:], z[k][:], z[k][:], ALU.mult)
+            nc.vector.scalar_tensor_tensor(
+                square_less_c2[k][:], x_sb[:], 2.0 * CENTERS[k], x_sb[:], ALU.subtract, ALU.mult
+            )
 
         tanh_half = held.tile([I, N], F32, name="tanh_half")
         nc.scalar.activation(tanh_half[:], x_sb[:], ACT.Tanh, scale=0.5)
@@ -59,28 +58,32 @@ def tile_kanlayer_kernel(tc, base, x, coeff, ew, bw, bb, offs, out):
         nc.vector.tensor_tensor(ew_bw[:], ew_sb[:], bw_sb[:], ALU.mult)
         ew_bb = held.tile([I, C], BF16, name="ew_bb")
         nc.vector.tensor_tensor(ew_bb[:], ew_sb[:], bb_sb[:], ALU.mult)
-        sigmoid = held.tile([I, N], F32, name="sigmoid")
-        nc.vector.tensor_scalar(sigmoid[:], tanh_half[:], 0.5, 0.5, ALU.mult, ALU.add)
-        silu = held.tile([I, N], BF16, name="silu")
-        nc.vector.tensor_tensor(silu[:], x_sb[:], sigmoid[:], ALU.mult)
-        a_ps = psum.tile([C, N], F32, name="a_ps")
-        nc.tensor.matmul(a_ps[:], ew_bb[:], ones[:], start=True, stop=False)
-        nc.tensor.matmul(a_ps[:], ew_bw[:], silu[:], start=False, stop=True)
+        twice_silu = held.tile([I, N], BF16, name="twice_silu")
+        nc.vector.scalar_tensor_tensor(twice_silu[:], tanh_half[:], 1.0, x_sb[:], ALU.add, ALU.mult)
+        twice_a_ps = psum.tile([C, N], F32, name="twice_a_ps")
+        nc.tensor.matmul(twice_a_ps[:], ew_bb[:], twos[:], start=True, stop=False)
+        nc.tensor.matmul(twice_a_ps[:], ew_bw[:], twice_silu[:], start=False, stop=True)
 
         b_ps = psum.tile([C, N], F32, name="b_ps")
         for k in range(K):
-            if k not in vector_squares:
-                nc.scalar.activation(
-                    z_squared[k][:], x_sb[:], ACT.Square, bias=-Z_SCALE * CENTERS[k], scale=Z_SCALE
-                )
             bump = held.tile([I, N], BF16, name=f"bump{k}")
-            nc.scalar.activation(bump[:], z_squared[k][:], ACT.Exp, scale=-1.0)
+            if k in vector_squares:
+                nc.scalar.activation(
+                    bump[:], square_less_c2[k][:], ACT.Exp,
+                    bias=-((Z_SCALE * CENTERS[k]) ** 2), scale=-(Z_SCALE**2),
+                )
+            else:
+                z_squared = held.tile([I, N], F32, name=f"z_squared{k}")
+                nc.scalar.activation(
+                    z_squared[:], x_sb[:], ACT.Square, bias=-Z_SCALE * CENTERS[k], scale=Z_SCALE
+                )
+                nc.scalar.activation(bump[:], z_squared[:], ACT.Exp, scale=-1.0)
             ew_coeff = held.tile([I, C], BF16, name=f"ew_coeff{k}")
             nc.vector.tensor_tensor(ew_coeff[:], coeff_sb[k], ew_sb[:], ALU.mult)
             nc.tensor.matmul(b_ps[:], ew_coeff[:], bump[:], start=(k == 0), stop=(k == K - 1))
 
         a_sb = held.tile([C, N], F32, name="a_sb")
-        nc.scalar.copy(a_sb[:], a_ps[:])
+        nc.scalar.mul(a_sb[:], twice_a_ps[:], 0.5)
         b_sb = held.tile([C, N], F32, name="b_sb")
         nc.scalar.copy(b_sb[:], b_ps[:])
 

@@ -11,7 +11,7 @@ SPACING = 0.400001
 CENTERS = [(2 * k - 5) / 11 for k in range(K)]
 Z_SCALE = 1.0 / (SPACING * math.sqrt(2.0))
 COEFF_PIECES = (1, 2, 2, 2, 1)
-K_VECTOR_SQUARES = 2
+K_VECTOR_SQUARES = 4
 
 FLOPS = 2 * C * N * I * (K + 1)
 

@@ -37,10 +37,10 @@ def tile_kanlayer_kernel(tc, base, x, coeff, ew, bw, bb, offs, out):
             piece = held.tile([I, bumps, C], F32, name=f"coeff_piece{k0}")
             nc.sync.dma_start(piece[:], coeff_ikc[:, k0 : k0 + bumps, :])
             coeff_sb.extend(piece[:, m, :] for m in range(bumps))
-        offsets = held.tile([128, N // 16], U16, name="offsets")
-        nc.sync.dma_start(offsets[:], offs)
         window = held.tile([C, S], F32, name="window")
         nc.sync.dma_start(window[:], base)
+        offsets = held.tile([128, N // 16], U16, name="offsets")
+        nc.sync.dma_start(offsets[:], offs)
 
         twos = held.tile([I, N], BF16, name="twos")
         nc.gpsimd.memset(twos[:], 2.0)

@@ -10,7 +10,7 @@ C, I, S, N, K = 128, 128, 512, 128, 8
 SPACING = 0.400001
 CENTERS = [(2 * k - 5) / 11 for k in range(K)]
 Z_SCALE = 1.0 / (SPACING * math.sqrt(2.0))
-COEFF_PIECES = (1, 2, 2, 2, 1)
+COEFF_PIECES = (1, 2, 2, 1, 1, 1)
 K_VECTOR_SQUARES = 4
 
 FLOPS = 2 * C * N * I * (K + 1)

@@ -10,7 +10,6 @@ C, I, S, N, K = 128, 128, 512, 128, 8
 SPACING = 0.400001
 CENTERS = [(2 * k - 5) / 11 for k in range(K)]
 Z_SCALE = 1.0 / (SPACING * math.sqrt(2.0))
-COEFF_PIECES = (1, 2, 2, 1, 1, 1)
 K_VECTOR_SQUARES = 4
 
 FLOPS = 2 * C * N * I * (K + 1)
@@ -30,13 +29,11 @@ def tile_kanlayer_kernel(tc, base, x, coeff, ew, bw, bb, offs, out):
         nc.sync.dma_start(bw_sb[:], bw)
         bb_sb = held.tile([I, C], F32, name="bb_sb")
         nc.sync.dma_start(bb_sb[:], bb)
-        coeff_ikc = coeff.rearrange("k i c -> i k c")
         coeff_sb = []
-        for bumps in COEFF_PIECES:
-            k0 = len(coeff_sb)
-            piece = held.tile([I, bumps, C], F32, name=f"coeff_piece{k0}")
-            nc.sync.dma_start(piece[:], coeff_ikc[:, k0 : k0 + bumps, :])
-            coeff_sb.extend(piece[:, m, :] for m in range(bumps))
+        for k in range(K):
+            bump_coeff = held.tile([I, C], F32, name=f"coeff{k}")
+            nc.sync.dma_start(bump_coeff[:], coeff[k])
+            coeff_sb.append(bump_coeff)
         window = held.tile([C, S], F32, name="window")
         nc.sync.dma_start(window[:], base)
         offsets = held.tile([128, N // 16], U16, name="offsets")
@@ -79,7 +76,7 @@ def tile_kanlayer_kernel(tc, base, x, coeff, ew, bw, bb, offs, out):
                 )
                 nc.scalar.activation(bump[:], z_squared[:], ACT.Exp, scale=-1.0)
             ew_coeff = held.tile([I, C], BF16, name=f"ew_coeff{k}")
-            nc.vector.tensor_tensor(ew_coeff[:], coeff_sb[k], ew_sb[:], ALU.mult)
+            nc.vector.tensor_tensor(ew_coeff[:], coeff_sb[k][:], ew_sb[:], ALU.mult)
             nc.tensor.matmul(b_ps[:], ew_coeff[:], bump[:], start=(k == 0), stop=(k == K - 1))
 
         a_sb = held.tile([C, N], F32, name="a_sb")

@@ -10,6 +10,7 @@ C, I, S, N, K = 128, 128, 512, 128, 8
 SPACING = 0.400001
 CENTERS = [(2 * k - 5) / 11 for k in range(K)]
 Z_SCALE = 1.0 / (SPACING * math.sqrt(2.0))
+COEFF_PIECES = (2, 1, 1, 1, 1, 1, 1)
 K_VECTOR_SQUARES = 4
 
 FLOPS = 2 * C * N * I * (K + 1)
@@ -29,11 +30,13 @@ def tile_kanlayer_kernel(tc, base, x, coeff, ew, bw, bb, offs, out):
         nc.sync.dma_start(bw_sb[:], bw)
         bb_sb = held.tile([I, C], F32, name="bb_sb")
         nc.sync.dma_start(bb_sb[:], bb)
+        coeff_ikc = coeff.rearrange("k i c -> i k c")
         coeff_sb = []
-        for k in range(K):
-            bump_coeff = held.tile([I, C], F32, name=f"coeff{k}")
-            nc.sync.dma_start(bump_coeff[:], coeff[k])
-            coeff_sb.append(bump_coeff)
+        for bumps in COEFF_PIECES:
+            k0 = len(coeff_sb)
+            piece = held.tile([I, bumps, C], F32, name=f"coeff_piece{k0}")
+            nc.sync.dma_start(piece[:], coeff_ikc[:, k0 : k0 + bumps, :])
+            coeff_sb.extend(piece[:, m, :] for m in range(bumps))
         window = held.tile([C, S], F32, name="window")
         nc.sync.dma_start(window[:], base)
         offsets = held.tile([128, N // 16], U16, name="offsets")
@@ -76,7 +79,7 @@ def tile_kanlayer_kernel(tc, base, x, coeff, ew, bw, bb, offs, out):
                 )
                 nc.scalar.activation(bump[:], z_squared[:], ACT.Exp, scale=-1.0)
             ew_coeff = held.tile([I, C], BF16, name=f"ew_coeff{k}")
-            nc.vector.tensor_tensor(ew_coeff[:], coeff_sb[k][:], ew_sb[:], ALU.mult)
+            nc.vector.tensor_tensor(ew_coeff[:], coeff_sb[k], ew_sb[:], ALU.mult)
             nc.tensor.matmul(b_ps[:], ew_coeff[:], bump[:], start=(k == 0), stop=(k == K - 1))
 
         a_sb = held.tile([C, N], F32, name="a_sb")

@@ -11,7 +11,7 @@ SPACING = 0.400001
 CENTERS = [(2 * k - 5) / 11 for k in range(K)]
 Z_SCALE = 1.0 / (SPACING * math.sqrt(2.0))
 COEFF_PIECES = (2, 1, 1, 1, 1, 1, 1)
-K_VECTOR_SQUARES = 4
+K_VECTOR_SQUARES = 3
 
 FLOPS = 2 * C * N * I * (K + 1)
 

import math

import concourse.mybir as mybir

F32, BF16, U16 = mybir.dt.float32, mybir.dt.bfloat16, mybir.dt.uint16
ALU = mybir.AluOpType
ACT = mybir.ActivationFunctionType

C, I, S, N, K = 128, 128, 512, 128, 8
SPACING = 0.400001
CENTERS = [(2 * k - 5) / 11 for k in range(K)]
Z_SCALE = 1.0 / (SPACING * math.sqrt(2.0))
COEFF_PIECES = (2, 1, 1, 1, 1, 1, 1)
K_VECTOR_SQUARES = 3

FLOPS = 2 * C * N * I * (K + 1)


def tile_kanlayer_kernel(tc, base, x, coeff, ew, bw, bb, offs, out):
    nc = tc.nc
    with (
        tc.tile_pool(name="held", bufs=1) as held,
        tc.psum_pool(name="psum", bufs=1) as psum,
    ):
        x_sb = held.tile([I, N], F32, name="x_sb")
        nc.sync.dma_start(x_sb[:], x)
        ew_sb = held.tile([I, C], F32, name="ew_sb")
        nc.sync.dma_start(ew_sb[:], ew)
        bw_sb = held.tile([I, C], F32, name="bw_sb")
        nc.sync.dma_start(bw_sb[:], bw)
        bb_sb = held.tile([I, C], F32, name="bb_sb")
        nc.sync.dma_start(bb_sb[:], bb)
        coeff_ikc = coeff.rearrange("k i c -> i k c")
        coeff_sb = []
        for bumps in COEFF_PIECES:
            k0 = len(coeff_sb)
            piece = held.tile([I, bumps, C], F32, name=f"coeff_piece{k0}")
            nc.sync.dma_start(piece[:], coeff_ikc[:, k0 : k0 + bumps, :])
            coeff_sb.extend(piece[:, m, :] for m in range(bumps))
        window = held.tile([C, S], F32, name="window")
        nc.sync.dma_start(window[:], base)
        offsets = held.tile([128, N // 16], U16, name="offsets")
        nc.sync.dma_start(offsets[:], offs)

        twos = held.tile([I, N], BF16, name="twos")
        nc.gpsimd.memset(twos[:], 2.0)

        vector_squares = range(K - K_VECTOR_SQUARES, K)
        square_less_c2 = {k: held.tile([I, N], F32, name=f"square_less_c2_{k}") for k in vector_squares}
        for k in vector_squares:
            nc.vector.scalar_tensor_tensor(
                square_less_c2[k][:], x_sb[:], 2.0 * CENTERS[k], x_sb[:], ALU.subtract, ALU.mult
            )

        tanh_half = held.tile([I, N], F32, name="tanh_half")
        nc.scalar.activation(tanh_half[:], x_sb[:], ACT.Tanh, scale=0.5)
        ew_bw = held.tile([I, C], BF16, name="ew_bw")
        nc.vector.tensor_tensor(ew_bw[:], ew_sb[:], bw_sb[:], ALU.mult)
        ew_bb = held.tile([I, C], BF16, name="ew_bb")
        nc.vector.tensor_tensor(ew_bb[:], ew_sb[:], bb_sb[:], ALU.mult)
        twice_silu = held.tile([I, N], BF16, name="twice_silu")
        nc.vector.scalar_tensor_tensor(twice_silu[:], tanh_half[:], 1.0, x_sb[:], ALU.add, ALU.mult)
        twice_a_ps = psum.tile([C, N], F32, name="twice_a_ps")
        nc.tensor.matmul(twice_a_ps[:], ew_bb[:], twos[:], start=True, stop=False)
        nc.tensor.matmul(twice_a_ps[:], ew_bw[:], twice_silu[:], start=False, stop=True)

        b_ps = psum.tile([C, N], F32, name="b_ps")
        for k in range(K):
            bump = held.tile([I, N], BF16, name=f"bump{k}")
            if k in vector_squares:
                nc.scalar.activation(
                    bump[:], square_less_c2[k][:], ACT.Exp,
                    bias=-((Z_SCALE * CENTERS[k]) ** 2), scale=-(Z_SCALE**2),
                )
            else:
                z_squared = held.tile([I, N], F32, name=f"z_squared{k}")
                nc.scalar.activation(
                    z_squared[:], x_sb[:], ACT.Square, bias=-Z_SCALE * CENTERS[k], scale=Z_SCALE
                )
                nc.scalar.activation(bump[:], z_squared[:], ACT.Exp, scale=-1.0)
            ew_coeff = held.tile([I, C], BF16, name=f"ew_coeff{k}")
            nc.vector.tensor_tensor(ew_coeff[:], coeff_sb[k], ew_sb[:], ALU.mult)
            nc.tensor.matmul(b_ps[:], ew_coeff[:], bump[:], start=(k == 0), stop=(k == K - 1))

        a_sb = held.tile([C, N], F32, name="a_sb")
        nc.scalar.mul(a_sb[:], twice_a_ps[:], 0.5)
        b_sb = held.tile([C, N], F32, name="b_sb")
        nc.scalar.copy(b_sb[:], b_ps[:])

        nc.vector.tensor_tensor(window[:].indirect(offsets[:]), a_sb[:], b_sb[:], ALU.add)
        nc.sync.dma_start(out, window[:])
